import numpy as np
import ml_dtypes


def mxq(x, axis, fmt="e4m3"):
    dtype, down = {"e4m3": (ml_dtypes.float8_e4m3fn, 7), "e5m2": (ml_dtypes.float8_e5m2, 14)}[fmt]
    v = np.moveaxis(np.asarray(x, np.float32).astype(ml_dtypes.bfloat16).astype(np.float64), axis, -1)
    blocks = v.reshape(v.shape[:-1] + (-1, 32))
    amax = np.abs(blocks).max(-1, keepdims=True)
    byte = np.maximum(np.where(amax > 0, np.frexp(amax)[1] - 1 + 127, 0) - down, 1)
    scale = np.exp2(byte - 127.0)
    codes = (blocks / scale).astype(np.float32).astype(dtype).astype(np.float64)
    return np.moveaxis((codes * scale).reshape(v.shape), -1, axis)


WIDE = False


def mx_kscale(k):
    if not WIDE:
        return np.ones(k)
    levels = np.array([10, -10, 5, -5, 0])
    a = np.random.permutation(np.resize(levels, k // 512 * 4)).reshape(k // 512, 4)
    idx = np.arange(k)
    return np.exp2(a[idx // 512, idx % 128 // 32])


BF16 = ml_dtypes.bfloat16


def bf(x):
    return np.asarray(x, np.float32).astype(BF16)


def f64(x):
    return np.asarray(x).astype(np.float64)


B, S, K, N = 4, 2048, 1024, 128
FP8_MAX = 448.0
EPS = 1e-12


def setup_inputs():
    s = mx_kscale(K)
    return {"x": bf(np.random.standard_normal((B, S, K)) * s),
            "weight": bf(np.random.standard_normal((K, N)) * 1.28 / np.sqrt(K) / s[:, None])}


def reference(x, weight):
    x = f64(x)
    weight = f64(weight)
    b, sl, k = x.shape
    n = weight.shape[1]
    x2 = x.reshape(-1, k)
    x_scale = FP8_MAX / np.maximum(np.max(np.abs(x2)), EPS)
    w_scale = FP8_MAX / np.maximum(np.max(np.abs(weight)), EPS)
    x_sim = np.clip(x2 * x_scale, -FP8_MAX, FP8_MAX)
    w_sim = np.clip(weight * w_scale, -FP8_MAX, FP8_MAX)
    out = (mxq(x_sim, 1, "e4m3") @ mxq(w_sim, 0, "e4m3")) * (1.0 / (x_scale * w_scale))
    return out.reshape(b, sl, n)

@@ -1,0 +1,205 @@
+from contextlib import ExitStack
+
+import concourse.mybir as mybir
+from concourse.masks import make_identity
+
+F32 = mybir.dt.float32
+BF16 = mybir.dt.bfloat16
+I32 = mybir.dt.int32
+U32 = mybir.dt.uint32
+U8 = mybir.dt.uint8
+FP8X4 = mybir.dt.float8_e4m3fn_x4
+ALU = mybir.AluOpType
+ACT = mybir.ActivationFunctionType
+AX = mybir.AxisListType
+
+P = 128
+ROWS = 8192
+K = 1024
+N_OUT = 128
+ROW_TILES = ROWS // P
+TILES_PER_CHUNK = 4
+CHUNKS = ROW_TILES // TILES_PER_CHUNK
+CHUNK_COLS = TILES_PER_CHUNK * K
+PASSES = K // 512
+ABS_MASK = 0x7FFF7FFF
+FP8_MAX = 448.0
+EPS = 1e-12
+SCALAR_ABS_COLS = 896
+SCALAR_SCALE_COLS = 1280
+
+FLOPS = 2 * ROWS * K * N_OUT
+
+
+def tile_modelnew_t_kernel(tc, x, weight, out):
+    nc = tc.nc
+    x_flat = x.flatten_outer_dims().rearrange("(p t) k -> p (t k)", t=ROW_TILES)
+    out_flat = out.flatten_outer_dims().rearrange("(p t) n -> p (t n)", t=ROW_TILES)
+
+    with ExitStack() as stack:
+        keep = stack.enter_context(tc.tile_pool(name="keep", bufs=1))
+        natural_pool = stack.enter_context(tc.tile_pool(name="natural", bufs=4))
+        tree_pool = stack.enter_context(tc.tile_pool(name="tree", bufs=2))
+        mx_pool = stack.enter_context(tc.tile_pool(name="mx", bufs=3))
+        result_pool = stack.enter_context(tc.tile_pool(name="result", bufs=3))
+        banks = stack.enter_context(tc.psum_pool(name="banks", bufs=8))
+        stack.enter_context(tc.manual_schedule())
+
+        w_raw = keep.tile([P, 2 * PASSES, 2 * N_OUT], BF16)
+        nc.sync.dma_start(out=w_raw[:], in_=weight.rearrange("(a p e) n -> p a (e n)", a=2 * PASSES, p=P, e=2))
+
+        identity = keep.tile([P, P], F32)
+        make_identity(nc, identity[:])
+        ones = keep.tile([P, P], F32)
+        nc.vector.memset(ones[:], 1.0)
+
+        def inverse_scale_of(column, name):
+            repeated = keep.tile([P, P], F32, name=name + "_repeated")
+            nc.vector.tensor_scalar(out=repeated[:], in0=ones[:], scalar1=column[:, 0:1], scalar2=None, op0=ALU.mult)
+            turned = banks.tile([P, P], F32, name=name + "_turned", tag="bank")
+            nc.tensor.transpose(turned[:], repeated[:], identity[:])
+            whole = keep.tile([P, 1], F32, name=name + "_whole")
+            nc.vector.reduce_max(out=whole[:], in_=turned[:], axis=AX.X)
+            inverse_scale = keep.tile([P, 1], F32, name=name + "_inverse_scale")
+            nc.vector.tensor_scalar(
+                out=inverse_scale[:], in0=whole[:], scalar1=EPS, scalar2=1.0 / FP8_MAX, op0=ALU.max, op1=ALU.mult
+            )
+            return inverse_scale
+
+        w_flat = w_raw[:].rearrange("p a c -> p (a c)")
+        w_abs = keep.tile([P, K], BF16)
+        nc.vector.tensor_scalar(
+            out=w_abs[:].bitcast(I32), in0=w_flat.bitcast(I32), scalar1=ABS_MASK, scalar2=None, op0=ALU.bitwise_and
+        )
+        w_column = keep.tile([P, 1], F32)
+        nc.vector.reduce_max(out=w_column[:], in_=w_abs[:], axis=AX.X)
+        w_inverse_scale = inverse_scale_of(w_column, "w")
+        w_scale = keep.tile([P, 1], F32)
+        nc.vector.reciprocal(out=w_scale[:], in_=w_inverse_scale[:])
+        w_grouped = keep.tile([P, PASSES, N_OUT, 4], BF16, align_bytes=64)
+        for g in range(PASSES):
+            nc.vector.tensor_scalar(
+                out=w_grouped[:, g].rearrange("p n (u e) -> p n u e", u=2),
+                in0=w_raw[:, 2 * g : 2 * g + 2, :].rearrange("p u (e n) -> p n u e", e=2),
+                scalar1=w_scale[:, 0:1],
+                scalar2=None,
+                op0=ALU.mult,
+            )
+        w_codes = keep.tile([P, PASSES * N_OUT], U32, align_bytes=64)
+        w_scales = keep.tile([P, PASSES * N_OUT], U8, align_bytes=64)
+        nc.vector.quantize_mx(
+            out=w_codes[:].bitcast(FP8X4), scales=w_scales[:], in_=w_grouped[:].rearrange("p g n j -> p (g n j)")
+        )
+
+        running = keep.tile([P, CHUNK_COLS // 4], BF16)
+        nc.vector.memset(running[:], 0.0)
+        grouped = []
+        magnitudes = {}
+        halves = {}
+        quarters = {}
+        for s in range(CHUNKS + 3):
+            if s < CHUNKS:
+                natural = natural_pool.tile([P, CHUNK_COLS], BF16, name="natural")
+                nc.sync.dma_start(out=natural[:], in_=x_flat[:, s * CHUNK_COLS : (s + 1) * CHUNK_COLS])
+                words = natural[:].bitcast(F32)
+                magnitude = tree_pool.tile([P, CHUNK_COLS], BF16, name="magnitude")
+                magnitudes[s] = magnitude
+                nc.scalar.activation(out=magnitude[:, :SCALAR_ABS_COLS], in_=natural[:, :SCALAR_ABS_COLS], func=ACT.Abs)
+                nc.vector.tensor_scalar(
+                    out=magnitude[:, SCALAR_ABS_COLS:].bitcast(I32),
+                    in0=natural[:, SCALAR_ABS_COLS:].bitcast(I32),
+                    scalar1=ABS_MASK,
+                    scalar2=None,
+                    op0=ALU.bitwise_and,
+                )
+                chunk = keep.tile([P, CHUNK_COLS], BF16, name="grouped%d" % s, align_bytes=64)
+                grouped.append(chunk)
+                chunk_words = chunk[:].bitcast(F32).rearrange(
+                    "p (t g r u) -> p t g r u", t=TILES_PER_CHUNK, g=PASSES, r=P, u=2
+                )
+                for t in range(TILES_PER_CHUNK):
+                    flipped = banks.tile([P, 2 * PASSES, P], F32, name="flipped", tag="bank")
+                    for a in range(2 * PASSES):
+                        first_word = t * (K // 2) + a * P
+                        nc.tensor.transpose(flipped[:, a, :], words[:, first_word : first_word + P], identity[:])
+                    nc.scalar.copy(out=chunk_words[:, t], in_=flipped[:].rearrange("p (g u) r -> p g r u", u=2))
+            if 1 <= s < CHUNKS + 1:
+                magnitude = magnitudes[s - 1]
+                half = tree_pool.tile([P, CHUNK_COLS // 2], BF16, name="half")
+                halves[s - 1] = half
+                nc.vector.tensor_tensor(
+                    out=half[:], in0=magnitude[:, : CHUNK_COLS // 2], in1=magnitude[:, CHUNK_COLS // 2 :], op=ALU.max
+                )
+            if 2 <= s < CHUNKS + 2:
+                half = halves[s - 2]
+                quarter = tree_pool.tile([P, CHUNK_COLS // 4], BF16, name="quarter")
+                quarters[s - 2] = quarter
+                nc.vector.tensor_tensor(
+                    out=quarter[:], in0=half[:, : CHUNK_COLS // 4], in1=half[:, CHUNK_COLS // 4 :], op=ALU.max
+                )
+            if 3 <= s:
+                nc.vector.tensor_tensor(out=running[:], in0=running[:], in1=quarters[s - 3][:], op=ALU.max)
+
+        narrow = keep.tile([P, CHUNK_COLS // 8], BF16)
+        nc.vector.tensor_tensor(
+            out=narrow[:], in0=running[:, : CHUNK_COLS // 8], in1=running[:, CHUNK_COLS // 8 :], op=ALU.max
+        )
+        x_column = keep.tile([P, 1], F32)
+        nc.vector.reduce_max(out=x_column[:], in_=narrow[:], axis=AX.X)
+        x_inverse_scale = inverse_scale_of(x_column, "x")
+        x_scale = keep.tile([P, 1], F32)
+        nc.vector.reciprocal(out=x_scale[:], in_=x_inverse_scale[:])
+        final_factor = keep.tile([P, 1], F32)
+
+        def scale(c):
+            flat = grouped[c]
+            nc.scalar.activation(
+                out=flat[:, :SCALAR_SCALE_COLS], in_=flat[:, :SCALAR_SCALE_COLS], func=ACT.Copy, scale=x_scale[:, 0:1]
+            )
+            nc.vector.tensor_scalar(
+                out=flat[:, SCALAR_SCALE_COLS:],
+                in0=flat[:, SCALAR_SCALE_COLS:],
+                scalar1=x_scale[:, 0:1],
+                scalar2=None,
+                op0=ALU.mult,
+            )
+
+        def multiply(c):
+            codes = mx_pool.tile([P, CHUNK_COLS // 4], U32, name="codes", align_bytes=64)
+            scales = mx_pool.tile([P, CHUNK_COLS // 4], U8, name="scales", align_bytes=64)
+            nc.vector.quantize_mx(out=codes[:].bitcast(FP8X4), scales=scales[:], in_=grouped[c][:])
+            acc = banks.tile([P, TILES_PER_CHUNK, N_OUT], F32, name="acc", tag="bank")
+            for t in range(TILES_PER_CHUNK):
+                for g in range(PASSES):
+                    x_cols = slice((t * PASSES + g) * P, (t * PASSES + g + 1) * P)
+                    w_cols = slice(g * N_OUT, (g + 1) * N_OUT)
+                    nc.tensor.matmul_mx(
+                        out=acc[:, t, :],
+                        lhsT=codes[:, x_cols].bitcast(FP8X4),
+                        lhsT_scale=scales[:, x_cols],
+                        rhs=w_codes[:, w_cols].bitcast(FP8X4),
+                        rhs_scale=w_scales[:, w_cols],
+                        start=(g == 0),
+                        stop=(g == PASSES - 1),
+                    )
+            return acc
+
+        def finish(c, acc):
+            result = result_pool.tile([P, TILES_PER_CHUNK * N_OUT], F32, name="result")
+            nc.scalar.activation(
+                out=result[:], in_=acc[:].rearrange("p t n -> p (t n)"), func=ACT.Copy, scale=final_factor[:, 0:1]
+            )
+            width = TILES_PER_CHUNK * N_OUT
+            nc.sync.dma_start(out=out_flat[:, c * width : (c + 1) * width], in_=result[:])
+
+        scale(0)
+        nc.vector.tensor_tensor(out=final_factor[:], in0=x_inverse_scale[:], in1=w_inverse_scale[:], op=ALU.mult)
+        scale(1)
+        products = {}
+        for c in range(CHUNKS):
+            products[c] = multiply(c)
+            if c + 2 < CHUNKS:
+                scale(c + 2)
+            if c >= 1:
+                finish(c - 1, products[c - 1])
+        finish(CHUNKS - 1, products[CHUNKS - 1])

@@ -25,7 +25,7 @@ PASSES = K // 512
 ABS_MASK = 0x7FFF7FFF
 FP8_MAX = 448.0
 EPS = 1e-12
-SCALAR_ABS_COLS = 896
+SCALAR_ABS_COLS = 768
 SCALAR_SCALE_COLS = 1280
 
 FLOPS = 2 * ROWS * K * N_OUT
@@ -46,109 +46,191 @@ def tile_modelnew_t_kernel(tc, x, weight, out):
         stack.enter_context(tc.manual_schedule())
 
         w_raw = keep.tile([P, 2 * PASSES, 2 * N_OUT], BF16)
-        nc.sync.dma_start(out=w_raw[:], in_=weight.rearrange("(a p e) n -> p a (e n)", a=2 * PASSES, p=P, e=2))
-
         identity = keep.tile([P, P], F32)
         make_identity(nc, identity[:])
-        ones = keep.tile([P, P], F32)
-        nc.vector.memset(ones[:], 1.0)
+        over_448 = keep.tile([P, P], F32)
+        nc.vector.memset(over_448[:], 1.0 / FP8_MAX)
+        running = keep.tile([P, CHUNK_COLS // 4], BF16)
+        nc.vector.memset(running[:], 0.0)
 
-        def inverse_scale_of(column, name):
+        def spread(column, name):
             repeated = keep.tile([P, P], F32, name=name + "_repeated")
-            nc.vector.tensor_scalar(out=repeated[:], in0=ones[:], scalar1=column[:, 0:1], scalar2=None, op0=ALU.mult)
+            nc.vector.tensor_scalar(
+                out=repeated[:], in0=over_448[:], scalar1=column[:, 0:1], scalar2=EPS / FP8_MAX, op0=ALU.mult, op1=ALU.max
+            )
             turned = banks.tile([P, P], F32, name=name + "_turned", tag="bank")
             nc.tensor.transpose(turned[:], repeated[:], identity[:])
-            whole = keep.tile([P, 1], F32, name=name + "_whole")
-            nc.vector.reduce_max(out=whole[:], in_=turned[:], axis=AX.X)
+            return turned
+
+        def inverse_scale_of(turned, name):
             inverse_scale = keep.tile([P, 1], F32, name=name + "_inverse_scale")
-            nc.vector.tensor_scalar(
-                out=inverse_scale[:], in0=whole[:], scalar1=EPS, scalar2=1.0 / FP8_MAX, op0=ALU.max, op1=ALU.mult
-            )
+            nc.vector.reduce_max(out=inverse_scale[:], in_=turned[:], axis=AX.X)
             return inverse_scale
+
+        def reciprocal_of(inverse_scale, name):
+            the_scale = keep.tile([P, 1], F32, name=name + "_scale")
+            nc.vector.reciprocal(out=the_scale[:], in_=inverse_scale[:])
+            return the_scale
 
         w_flat = w_raw[:].rearrange("p a c -> p (a c)")
         w_abs = keep.tile([P, K], BF16)
-        nc.vector.tensor_scalar(
-            out=w_abs[:].bitcast(I32), in0=w_flat.bitcast(I32), scalar1=ABS_MASK, scalar2=None, op0=ALU.bitwise_and
-        )
+        w_half = keep.tile([P, K // 2], BF16)
         w_column = keep.tile([P, 1], F32)
-        nc.vector.reduce_max(out=w_column[:], in_=w_abs[:], axis=AX.X)
-        w_inverse_scale = inverse_scale_of(w_column, "w")
-        w_scale = keep.tile([P, 1], F32)
-        nc.vector.reciprocal(out=w_scale[:], in_=w_inverse_scale[:])
         w_grouped = keep.tile([P, PASSES, N_OUT, 4], BF16, align_bytes=64)
-        for g in range(PASSES):
+        w_codes = keep.tile([P, PASSES * N_OUT], U32, align_bytes=64)
+        w_scales = keep.tile([P, PASSES * N_OUT], U8, align_bytes=64)
+        w_facts = {}
+
+        def weight_magnitude():
+            nc.vector.tensor_scalar(
+                out=w_abs[:].bitcast(I32), in0=w_flat.bitcast(I32), scalar1=ABS_MASK, scalar2=None, op0=ALU.bitwise_and
+            )
+
+        def weight_half():
+            nc.vector.tensor_tensor(out=w_half[:], in0=w_abs[:, : K // 2], in1=w_abs[:, K // 2 :], op=ALU.max)
+
+        def weight_column():
+            nc.vector.reduce_max(out=w_column[:], in_=w_half[:], axis=AX.X)
+
+        def weight_group(g):
             nc.vector.tensor_scalar(
                 out=w_grouped[:, g].rearrange("p n (u e) -> p n u e", u=2),
                 in0=w_raw[:, 2 * g : 2 * g + 2, :].rearrange("p u (e n) -> p n u e", e=2),
-                scalar1=w_scale[:, 0:1],
+                scalar1=w_facts["scale"][:, 0:1],
                 scalar2=None,
                 op0=ALU.mult,
             )
-        w_codes = keep.tile([P, PASSES * N_OUT], U32, align_bytes=64)
-        w_scales = keep.tile([P, PASSES * N_OUT], U8, align_bytes=64)
-        nc.vector.quantize_mx(
-            out=w_codes[:].bitcast(FP8X4), scales=w_scales[:], in_=w_grouped[:].rearrange("p g n j -> p (g n j)")
-        )
 
-        running = keep.tile([P, CHUNK_COLS // 4], BF16)
-        nc.vector.memset(running[:], 0.0)
+        def weight_quantise():
+            nc.vector.quantize_mx(
+                out=w_codes[:].bitcast(FP8X4), scales=w_scales[:], in_=w_grouped[:].rearrange("p g n j -> p (g n j)")
+            )
+
         grouped = []
+        naturals = {}
         magnitudes = {}
         halves = {}
         quarters = {}
-        for s in range(CHUNKS + 3):
-            if s < CHUNKS:
-                natural = natural_pool.tile([P, CHUNK_COLS], BF16, name="natural")
-                nc.sync.dma_start(out=natural[:], in_=x_flat[:, s * CHUNK_COLS : (s + 1) * CHUNK_COLS])
-                words = natural[:].bitcast(F32)
-                magnitude = tree_pool.tile([P, CHUNK_COLS], BF16, name="magnitude")
-                magnitudes[s] = magnitude
-                nc.scalar.activation(out=magnitude[:, :SCALAR_ABS_COLS], in_=natural[:, :SCALAR_ABS_COLS], func=ACT.Abs)
-                nc.vector.tensor_scalar(
-                    out=magnitude[:, SCALAR_ABS_COLS:].bitcast(I32),
-                    in0=natural[:, SCALAR_ABS_COLS:].bitcast(I32),
-                    scalar1=ABS_MASK,
-                    scalar2=None,
-                    op0=ALU.bitwise_and,
-                )
-                chunk = keep.tile([P, CHUNK_COLS], BF16, name="grouped%d" % s, align_bytes=64)
-                grouped.append(chunk)
-                chunk_words = chunk[:].bitcast(F32).rearrange(
-                    "p (t g r u) -> p t g r u", t=TILES_PER_CHUNK, g=PASSES, r=P, u=2
-                )
-                for t in range(TILES_PER_CHUNK):
-                    flipped = banks.tile([P, 2 * PASSES, P], F32, name="flipped", tag="bank")
-                    for a in range(2 * PASSES):
-                        first_word = t * (K // 2) + a * P
-                        nc.tensor.transpose(flipped[:, a, :], words[:, first_word : first_word + P], identity[:])
-                    nc.scalar.copy(out=chunk_words[:, t], in_=flipped[:].rearrange("p (g u) r -> p g r u", u=2))
-            if 1 <= s < CHUNKS + 1:
-                magnitude = magnitudes[s - 1]
-                half = tree_pool.tile([P, CHUNK_COLS // 2], BF16, name="half")
-                halves[s - 1] = half
-                nc.vector.tensor_tensor(
-                    out=half[:], in0=magnitude[:, : CHUNK_COLS // 2], in1=magnitude[:, CHUNK_COLS // 2 :], op=ALU.max
-                )
-            if 2 <= s < CHUNKS + 2:
-                half = halves[s - 2]
-                quarter = tree_pool.tile([P, CHUNK_COLS // 4], BF16, name="quarter")
-                quarters[s - 2] = quarter
-                nc.vector.tensor_tensor(
-                    out=quarter[:], in0=half[:, : CHUNK_COLS // 4], in1=half[:, CHUNK_COLS // 4 :], op=ALU.max
-                )
-            if 3 <= s:
-                nc.vector.tensor_tensor(out=running[:], in0=running[:], in1=quarters[s - 3][:], op=ALU.max)
+        flipped_banks = {}
 
-        narrow = keep.tile([P, CHUNK_COLS // 8], BF16)
-        nc.vector.tensor_tensor(
-            out=narrow[:], in0=running[:, : CHUNK_COLS // 8], in1=running[:, CHUNK_COLS // 8 :], op=ALU.max
-        )
+        def load_and_transpose(s):
+            natural = natural_pool.tile([P, CHUNK_COLS], BF16, name="natural")
+            naturals[s] = natural
+            pieces = TILES_PER_CHUNK if s == 0 else 1
+            width = CHUNK_COLS // pieces
+            for i in range(pieces):
+                nc.sync.dma_start(
+                    out=natural[:, i * width : (i + 1) * width],
+                    in_=x_flat[:, s * CHUNK_COLS + i * width : s * CHUNK_COLS + (i + 1) * width],
+                )
+            if s == 3:
+                nc.sync.dma_start(out=w_raw[:], in_=weight.rearrange("(a p e) n -> p a (e n)", a=2 * PASSES, p=P, e=2))
+            words = natural[:].bitcast(F32)
+            for t in range(TILES_PER_CHUNK):
+                flipped = banks.tile([P, 2 * PASSES, P], F32, name="flipped", tag="bank")
+                flipped_banks[(s, t)] = flipped
+                for a in range(2 * PASSES):
+                    first_word = t * (K // 2) + a * P
+                    nc.tensor.transpose(flipped[:, a, :], words[:, first_word : first_word + P], identity[:])
+
+        def copy_out(s):
+            chunk = keep.tile([P, CHUNK_COLS], BF16, name="grouped%d" % s, align_bytes=64)
+            grouped.append(chunk)
+            chunk_words = chunk[:].bitcast(F32).rearrange(
+                "p (t g r u) -> p t g r u", t=TILES_PER_CHUNK, g=PASSES, r=P, u=2
+            )
+            for t in range(TILES_PER_CHUNK):
+                nc.scalar.copy(
+                    out=chunk_words[:, t], in_=flipped_banks[(s, t)][:].rearrange("p (g u) r -> p g r u", u=2)
+                )
+
+        def magnitude_of(s):
+            natural = naturals[s]
+            magnitude = tree_pool.tile([P, CHUNK_COLS], BF16, name="magnitude")
+            magnitudes[s] = magnitude
+            nc.scalar.activation(out=magnitude[:, :SCALAR_ABS_COLS], in_=natural[:, :SCALAR_ABS_COLS], func=ACT.Abs)
+            nc.vector.tensor_scalar(
+                out=magnitude[:, SCALAR_ABS_COLS:].bitcast(I32),
+                in0=natural[:, SCALAR_ABS_COLS:].bitcast(I32),
+                scalar1=ABS_MASK,
+                scalar2=None,
+                op0=ALU.bitwise_and,
+            )
+
+        def fold_half(s):
+            magnitude = magnitudes[s]
+            half = tree_pool.tile([P, CHUNK_COLS // 2], BF16, name="half")
+            halves[s] = half
+            nc.vector.tensor_tensor(
+                out=half[:], in0=magnitude[:, : CHUNK_COLS // 2], in1=magnitude[:, CHUNK_COLS // 2 :], op=ALU.max
+            )
+
+        def fold_quarter(s):
+            half = halves[s]
+            quarter = tree_pool.tile([P, CHUNK_COLS // 4], BF16, name="quarter")
+            quarters[s] = quarter
+            nc.vector.tensor_tensor(
+                out=quarter[:], in0=half[:, : CHUNK_COLS // 4], in1=half[:, CHUNK_COLS // 4 :], op=ALU.max
+            )
+
+        def fold_running(s):
+            nc.vector.tensor_tensor(out=running[:], in0=running[:], in1=quarters[s][:], op=ALU.max)
+
+        load_and_transpose(0)
+        first_magnitude = tree_pool.tile([P, CHUNK_COLS], BF16, name="magnitude")
+
+        def first_mask(i):
+            nc.vector.tensor_scalar(
+                out=first_magnitude[:, i * K : (i + 1) * K].bitcast(I32),
+                in0=naturals[0][:, i * K : (i + 1) * K].bitcast(I32),
+                scalar1=ABS_MASK,
+                scalar2=None,
+                op0=ALU.bitwise_and,
+            )
+
+        def first_fold(i):
+            nc.vector.tensor_tensor(
+                out=running[:], in0=running[:], in1=first_magnitude[:, i * K : (i + 1) * K], op=ALU.max
+            )
+
+        first_mask(0)
+        first_mask(1)
+        first_fold(0)
+        first_mask(2)
+        first_fold(1)
+        first_mask(3)
+        first_fold(2)
+        for s in range(1, CHUNKS):
+            load_and_transpose(s)
+            if s >= 2:
+                fold_half(s - 1)
+            magnitude_of(s)
+            copy_out(s - 1)
+            if s == 1:
+                first_fold(3)
+            if s >= 2:
+                fold_quarter(s - 1)
+            if s >= 3:
+                fold_running(s - 2)
+        copy_out(CHUNKS - 1)
+        fold_half(CHUNKS - 1)
+        weight_magnitude()
+        fold_quarter(CHUNKS - 1)
+        weight_half()
+        fold_running(CHUNKS - 2)
+        weight_column()
+        fold_running(CHUNKS - 1)
+        w_turned = spread(w_column, "w")
         x_column = keep.tile([P, 1], F32)
-        nc.vector.reduce_max(out=x_column[:], in_=narrow[:], axis=AX.X)
-        x_inverse_scale = inverse_scale_of(x_column, "x")
-        x_scale = keep.tile([P, 1], F32)
-        nc.vector.reciprocal(out=x_scale[:], in_=x_inverse_scale[:])
+        nc.vector.reduce_max(out=x_column[:], in_=running[:], axis=AX.X)
+        w_facts["inverse_scale"] = inverse_scale_of(w_turned, "w")
+        x_turned = spread(x_column, "x")
+        w_facts["scale"] = reciprocal_of(w_facts["inverse_scale"], "w")
+        weight_group(0)
+        weight_group(1)
+        x_inverse_scale = inverse_scale_of(x_turned, "x")
+        weight_quantise()
+        x_scale = reciprocal_of(x_inverse_scale, "x")
         final_factor = keep.tile([P, 1], F32)
 
         def scale(c):
@@ -164,12 +246,15 @@ def tile_modelnew_t_kernel(tc, x, weight, out):
                 op0=ALU.mult,
             )
 
-        def multiply(c):
-            codes = mx_pool.tile([P, CHUNK_COLS // 4], U32, name="codes", align_bytes=64)
-            scales = mx_pool.tile([P, CHUNK_COLS // 4], U8, name="scales", align_bytes=64)
-            nc.vector.quantize_mx(out=codes[:].bitcast(FP8X4), scales=scales[:], in_=grouped[c][:])
-            acc = banks.tile([P, TILES_PER_CHUNK, N_OUT], F32, name="acc", tag="bank")
-            for t in range(TILES_PER_CHUNK):
+        def multiply(c, first_tile, tiles):
+            width = tiles * K
+            codes = mx_pool.tile([P, width // 4], U32, name="codes", align_bytes=64)
+            scales = mx_pool.tile([P, width // 4], U8, name="scales", align_bytes=64)
+            nc.vector.quantize_mx(
+                out=codes[:].bitcast(FP8X4), scales=scales[:], in_=grouped[c][:, first_tile * K : first_tile * K + width]
+            )
+            acc = banks.tile([P, tiles, N_OUT], F32, name="acc", tag="bank")
+            for t in range(tiles):
                 for g in range(PASSES):
                     x_cols = slice((t * PASSES + g) * P, (t * PASSES + g + 1) * P)
                     w_cols = slice(g * N_OUT, (g + 1) * N_OUT)
@@ -184,22 +269,33 @@ def tile_modelnew_t_kernel(tc, x, weight, out):
                     )
             return acc
 
-        def finish(c, acc):
-            result = result_pool.tile([P, TILES_PER_CHUNK * N_OUT], F32, name="result")
+        def finish(c, first_tile, tiles, acc):
+            width = tiles * N_OUT
+            if tiles == TILES_PER_CHUNK:
+                result = result_pool.tile([P, width], F32, name="result")
+            else:
+                result = keep.tile([P, width], F32, name="piece%d" % first_tile)
             nc.scalar.activation(
                 out=result[:], in_=acc[:].rearrange("p t n -> p (t n)"), func=ACT.Copy, scale=final_factor[:, 0:1]
             )
-            width = TILES_PER_CHUNK * N_OUT
-            nc.sync.dma_start(out=out_flat[:, c * width : (c + 1) * width], in_=result[:])
+            first_col = (c * TILES_PER_CHUNK + first_tile) * N_OUT
+            nc.sync.dma_start(out=out_flat[:, first_col : first_col + width], in_=result[:])
 
         scale(0)
-        nc.vector.tensor_tensor(out=final_factor[:], in0=x_inverse_scale[:], in1=w_inverse_scale[:], op=ALU.mult)
+        nc.vector.tensor_tensor(out=final_factor[:], in0=x_inverse_scale[:], in1=w_facts["inverse_scale"][:], op=ALU.mult)
         scale(1)
         products = {}
-        for c in range(CHUNKS):
-            products[c] = multiply(c)
+        for c in range(CHUNKS - 1):
+            products[c] = multiply(c, 0, TILES_PER_CHUNK)
             if c + 2 < CHUNKS:
                 scale(c + 2)
             if c >= 1:
-                finish(c - 1, products[c - 1])
-        finish(CHUNKS - 1, products[CHUNKS - 1])
+                finish(c - 1, 0, TILES_PER_CHUNK, products[c - 1])
+        last = CHUNKS - 1
+        for t in range(TILES_PER_CHUNK):
+            products[(last, t)] = multiply(last, t, 1)
+            if t == 0:
+                finish(last - 1, 0, TILES_PER_CHUNK, products[last - 1])
+            else:
+                finish(last, t - 1, 1, products[(last, t - 1)])
+        finish(last, TILES_PER_CHUNK - 1, 1, products[(last, TILES_PER_CHUNK - 1)])

@@ -21,12 +21,16 @@ ROW_TILES = ROWS // P
 TILES_PER_CHUNK = 4
 CHUNKS = ROW_TILES // TILES_PER_CHUNK
 CHUNK_COLS = TILES_PER_CHUNK * K
+FLOW_TILES = TILES_PER_CHUNK - 1
+FLOW_COLS = FLOW_TILES * K
 PASSES = K // 512
+WORDS = K // 2
 ABS_MASK = 0x7FFF7FFF
 FP8_MAX = 448.0
 EPS = 1e-12
-SCALAR_ABS_COLS = 768
-SCALAR_SCALE_COLS = 1280
+EXTRA_ABS_COLS = 192
+EXTRA_SCALE_COLS = 192
+HELD_AHEAD = 3
 
 FLOPS = 2 * ROWS * K * N_OUT
 
@@ -45,12 +49,11 @@ def tile_modelnew_t_kernel(tc, x, weight, out):
         banks = stack.enter_context(tc.psum_pool(name="banks", bufs=8))
         stack.enter_context(tc.manual_schedule())
 
-        w_raw = keep.tile([P, 2 * PASSES, 2 * N_OUT], BF16)
         identity = keep.tile([P, P], F32)
         make_identity(nc, identity[:])
         over_448 = keep.tile([P, P], F32)
         nc.vector.memset(over_448[:], 1.0 / FP8_MAX)
-        running = keep.tile([P, CHUNK_COLS // 4], BF16)
+        running = keep.tile([P, K], BF16)
         nc.vector.memset(running[:], 0.0)
 
         def spread(column, name):
@@ -72,6 +75,18 @@ def tile_modelnew_t_kernel(tc, x, weight, out):
             nc.vector.reciprocal(out=the_scale[:], in_=inverse_scale[:])
             return the_scale
 
+        def clear_signs(out_cols, in_cols):
+            nc.vector.tensor_scalar(
+                out=out_cols.bitcast(I32), in0=in_cols.bitcast(I32), scalar1=ABS_MASK, scalar2=None, op0=ALU.bitwise_and
+            )
+
+        def transpose_tile(words):
+            flipped = banks.tile([P, WORDS], F32, name="flipped", tag="bank")
+            for a in range(2 * PASSES):
+                nc.tensor.transpose(flipped[:, a * P : (a + 1) * P], words[:, a * P : (a + 1) * P], identity[:])
+            return flipped
+
+        w_raw = keep.tile([P, 2 * PASSES, 2 * N_OUT], BF16)
         w_flat = w_raw[:].rearrange("p a c -> p (a c)")
         w_abs = keep.tile([P, K], BF16)
         w_half = keep.tile([P, K // 2], BF16)
@@ -79,31 +94,14 @@ def tile_modelnew_t_kernel(tc, x, weight, out):
         w_grouped = keep.tile([P, PASSES, N_OUT, 4], BF16, align_bytes=64)
         w_codes = keep.tile([P, PASSES * N_OUT], U32, align_bytes=64)
         w_scales = keep.tile([P, PASSES * N_OUT], U8, align_bytes=64)
-        w_facts = {}
 
-        def weight_magnitude():
-            nc.vector.tensor_scalar(
-                out=w_abs[:].bitcast(I32), in0=w_flat.bitcast(I32), scalar1=ABS_MASK, scalar2=None, op0=ALU.bitwise_and
-            )
-
-        def weight_half():
-            nc.vector.tensor_tensor(out=w_half[:], in0=w_abs[:, : K // 2], in1=w_abs[:, K // 2 :], op=ALU.max)
-
-        def weight_column():
-            nc.vector.reduce_max(out=w_column[:], in_=w_half[:], axis=AX.X)
-
-        def weight_group(g):
+        def weight_group(g, w_scale):
             nc.vector.tensor_scalar(
                 out=w_grouped[:, g].rearrange("p n (u e) -> p n u e", u=2),
                 in0=w_raw[:, 2 * g : 2 * g + 2, :].rearrange("p u (e n) -> p n u e", e=2),
-                scalar1=w_facts["scale"][:, 0:1],
+                scalar1=w_scale[:, 0:1],
                 scalar2=None,
                 op0=ALU.mult,
-            )
-
-        def weight_quantise():
-            nc.vector.quantize_mx(
-                out=w_codes[:].bitcast(FP8X4), scales=w_scales[:], in_=w_grouped[:].rearrange("p g n j -> p (g n j)")
             )
 
         grouped = []
@@ -111,51 +109,46 @@ def tile_modelnew_t_kernel(tc, x, weight, out):
         magnitudes = {}
         halves = {}
         quarters = {}
-        flipped_banks = {}
+        flow_banks = {}
+        held_banks = {}
 
         def load_and_transpose(s):
-            natural = natural_pool.tile([P, CHUNK_COLS], BF16, name="natural")
+            chunk = keep.tile([P, CHUNK_COLS], BF16, name="grouped%d" % s, align_bytes=64)
+            grouped.append(chunk)
+            natural = natural_pool.tile([P, FLOW_COLS], BF16, name="natural")
             naturals[s] = natural
-            pieces = TILES_PER_CHUNK if s == 0 else 1
-            width = CHUNK_COLS // pieces
+            first = s * CHUNK_COLS
+            nc.sync.dma_start(out=chunk[:, :K], in_=x_flat[:, first : first + K])
+            pieces = FLOW_TILES if s == 0 else 1
+            width = FLOW_COLS // pieces
             for i in range(pieces):
                 nc.sync.dma_start(
                     out=natural[:, i * width : (i + 1) * width],
-                    in_=x_flat[:, s * CHUNK_COLS + i * width : s * CHUNK_COLS + (i + 1) * width],
+                    in_=x_flat[:, first + K + i * width : first + K + (i + 1) * width],
                 )
-            if s == 3:
-                nc.sync.dma_start(out=w_raw[:], in_=weight.rearrange("(a p e) n -> p a (e n)", a=2 * PASSES, p=P, e=2))
             words = natural[:].bitcast(F32)
-            for t in range(TILES_PER_CHUNK):
-                flipped = banks.tile([P, 2 * PASSES, P], F32, name="flipped", tag="bank")
-                flipped_banks[(s, t)] = flipped
-                for a in range(2 * PASSES):
-                    first_word = t * (K // 2) + a * P
-                    nc.tensor.transpose(flipped[:, a, :], words[:, first_word : first_word + P], identity[:])
+            for t in range(FLOW_TILES):
+                flow_banks[(s, t)] = transpose_tile(words[:, t * WORDS : (t + 1) * WORDS])
 
         def copy_out(s):
-            chunk = keep.tile([P, CHUNK_COLS], BF16, name="grouped%d" % s, align_bytes=64)
-            grouped.append(chunk)
-            chunk_words = chunk[:].bitcast(F32).rearrange(
+            chunk_words = grouped[s][:].bitcast(F32).rearrange(
                 "p (t g r u) -> p t g r u", t=TILES_PER_CHUNK, g=PASSES, r=P, u=2
             )
-            for t in range(TILES_PER_CHUNK):
+            for t in range(FLOW_TILES):
                 nc.scalar.copy(
-                    out=chunk_words[:, t], in_=flipped_banks[(s, t)][:].rearrange("p (g u) r -> p g r u", u=2)
+                    out=chunk_words[:, t + 1],
+                    in_=flow_banks[(s, t)][:].rearrange("p (g u r) -> p g r u", g=PASSES, u=2, r=P),
                 )
 
         def magnitude_of(s):
             natural = naturals[s]
             magnitude = tree_pool.tile([P, CHUNK_COLS], BF16, name="magnitude")
             magnitudes[s] = magnitude
-            nc.scalar.activation(out=magnitude[:, :SCALAR_ABS_COLS], in_=natural[:, :SCALAR_ABS_COLS], func=ACT.Abs)
-            nc.vector.tensor_scalar(
-                out=magnitude[:, SCALAR_ABS_COLS:].bitcast(I32),
-                in0=natural[:, SCALAR_ABS_COLS:].bitcast(I32),
-                scalar1=ABS_MASK,
-                scalar2=None,
-                op0=ALU.bitwise_and,
+            nc.scalar.activation(out=magnitude[:, :K], in_=grouped[s][:, :K], func=ACT.Abs)
+            nc.scalar.activation(
+                out=magnitude[:, K : K + EXTRA_ABS_COLS], in_=natural[:, :EXTRA_ABS_COLS], func=ACT.Abs
             )
+            clear_signs(magnitude[:, K + EXTRA_ABS_COLS :], natural[:, EXTRA_ABS_COLS:])
 
         def fold_half(s):
             magnitude = magnitudes[s]
@@ -167,31 +160,23 @@ def tile_modelnew_t_kernel(tc, x, weight, out):
 
         def fold_quarter(s):
             half = halves[s]
-            quarter = tree_pool.tile([P, CHUNK_COLS // 4], BF16, name="quarter")
+            quarter = tree_pool.tile([P, K], BF16, name="quarter")
             quarters[s] = quarter
-            nc.vector.tensor_tensor(
-                out=quarter[:], in0=half[:, : CHUNK_COLS // 4], in1=half[:, CHUNK_COLS // 4 :], op=ALU.max
-            )
+            nc.vector.tensor_tensor(out=quarter[:], in0=half[:, :K], in1=half[:, K:], op=ALU.max)
 
-        def fold_running(s):
-            nc.vector.tensor_tensor(out=running[:], in0=running[:], in1=quarters[s][:], op=ALU.max)
+        def fold_running(values):
+            nc.vector.tensor_tensor(out=running[:], in0=running[:], in1=values, op=ALU.max)
 
         load_and_transpose(0)
+        nc.sync.dma_start(out=w_raw[:], in_=weight.rearrange("(a p e) n -> p a (e n)", a=2 * PASSES, p=P, e=2))
         first_magnitude = tree_pool.tile([P, CHUNK_COLS], BF16, name="magnitude")
 
         def first_mask(i):
-            nc.vector.tensor_scalar(
-                out=first_magnitude[:, i * K : (i + 1) * K].bitcast(I32),
-                in0=naturals[0][:, i * K : (i + 1) * K].bitcast(I32),
-                scalar1=ABS_MASK,
-                scalar2=None,
-                op0=ALU.bitwise_and,
-            )
+            source = grouped[0][:, :K] if i == 0 else naturals[0][:, (i - 1) * K : i * K]
+            clear_signs(first_magnitude[:, i * K : (i + 1) * K], source)
 
         def first_fold(i):
-            nc.vector.tensor_tensor(
-                out=running[:], in0=running[:], in1=first_magnitude[:, i * K : (i + 1) * K], op=ALU.max
-            )
+            fold_running(first_magnitude[:, i * K : (i + 1) * K])
 
         first_mask(0)
         first_mask(1)
@@ -200,6 +185,12 @@ def tile_modelnew_t_kernel(tc, x, weight, out):
         first_fold(1)
         first_mask(3)
         first_fold(2)
+        clear_signs(w_abs[:], w_flat)
+        first_fold(3)
+        nc.vector.tensor_tensor(out=w_half[:], in0=w_abs[:, : K // 2], in1=w_abs[:, K // 2 :], op=ALU.max)
+        nc.vector.reduce_max(out=w_column[:], in_=w_half[:], axis=AX.X)
+        w_turned = spread(w_column, "w")
+        w_facts = {}
         for s in range(1, CHUNKS):
             load_and_transpose(s)
             if s >= 2:
@@ -207,43 +198,52 @@ def tile_modelnew_t_kernel(tc, x, weight, out):
             magnitude_of(s)
             copy_out(s - 1)
             if s == 1:
-                first_fold(3)
+                w_facts["inverse_scale"] = inverse_scale_of(w_turned, "w")
             if s >= 2:
                 fold_quarter(s - 1)
+            if s == 2:
+                w_facts["scale"] = reciprocal_of(w_facts["inverse_scale"], "w")
             if s >= 3:
-                fold_running(s - 2)
+                fold_running(quarters[s - 2][:])
         copy_out(CHUNKS - 1)
+
+        def transpose_held(c):
+            held_banks[c] = transpose_tile(grouped[c][:, :K].bitcast(F32))
+
+        for c in range(HELD_AHEAD):
+            transpose_held(c)
         fold_half(CHUNKS - 1)
-        weight_magnitude()
+        fold_running(quarters[CHUNKS - 2][:])
         fold_quarter(CHUNKS - 1)
-        weight_half()
-        fold_running(CHUNKS - 2)
-        weight_column()
-        fold_running(CHUNKS - 1)
-        w_turned = spread(w_column, "w")
+        fold_running(quarters[CHUNKS - 1][:])
         x_column = keep.tile([P, 1], F32)
         nc.vector.reduce_max(out=x_column[:], in_=running[:], axis=AX.X)
-        w_facts["inverse_scale"] = inverse_scale_of(w_turned, "w")
         x_turned = spread(x_column, "x")
-        w_facts["scale"] = reciprocal_of(w_facts["inverse_scale"], "w")
-        weight_group(0)
-        weight_group(1)
+        weight_group(0, w_facts["scale"])
+        weight_group(1, w_facts["scale"])
         x_inverse_scale = inverse_scale_of(x_turned, "x")
-        weight_quantise()
+        nc.vector.quantize_mx(
+            out=w_codes[:].bitcast(FP8X4), scales=w_scales[:], in_=w_grouped[:].rearrange("p g n j -> p (g n j)")
+        )
         x_scale = reciprocal_of(x_inverse_scale, "x")
         final_factor = keep.tile([P, 1], F32)
+        nc.vector.tensor_tensor(out=final_factor[:], in0=x_inverse_scale[:], in1=w_facts["inverse_scale"][:], op=ALU.mult)
 
         def scale(c):
             flat = grouped[c]
-            nc.scalar.activation(
-                out=flat[:, :SCALAR_SCALE_COLS], in_=flat[:, :SCALAR_SCALE_COLS], func=ACT.Copy, scale=x_scale[:, 0:1]
-            )
+            pairs = held_banks[c][:].bitcast(BF16)
+            for g in range(PASSES):
+                cols = slice(g * 512, (g + 1) * 512)
+                nc.scalar.activation(
+                    out=flat[:, cols].rearrange("p (r u e) -> p r u e", r=P, u=2, e=2),
+                    in_=pairs[:, cols].rearrange("p (u r e) -> p r u e", u=2, r=P, e=2),
+                    func=ACT.Copy,
+                    scale=x_scale[:, 0:1],
+                )
+            split = K + EXTRA_SCALE_COLS
+            nc.scalar.activation(out=flat[:, K:split], in_=flat[:, K:split], func=ACT.Copy, scale=x_scale[:, 0:1])
             nc.vector.tensor_scalar(
-                out=flat[:, SCALAR_SCALE_COLS:],
-                in0=flat[:, SCALAR_SCALE_COLS:],
-                scalar1=x_scale[:, 0:1],
-                scalar2=None,
-                op0=ALU.mult,
+                out=flat[:, split:], in0=flat[:, split:], scalar1=x_scale[:, 0:1], scalar2=None, op0=ALU.mult
             )
 
         def multiply(c, first_tile, tiles):
@@ -282,11 +282,12 @@ def tile_modelnew_t_kernel(tc, x, weight, out):
             nc.sync.dma_start(out=out_flat[:, first_col : first_col + width], in_=result[:])
 
         scale(0)
-        nc.vector.tensor_tensor(out=final_factor[:], in0=x_inverse_scale[:], in1=w_facts["inverse_scale"][:], op=ALU.mult)
         scale(1)
         products = {}
         for c in range(CHUNKS - 1):
             products[c] = multiply(c, 0, TILES_PER_CHUNK)
+            if c + HELD_AHEAD < CHUNKS:
+                transpose_held(c + HELD_AHEAD)
             if c + 2 < CHUNKS:
                 scale(c + 2)
             if c >= 1:

@@ -29,8 +29,10 @@ ABS_MASK = 0x7FFF7FFF
 FP8_MAX = 448.0
 EPS = 1e-12
 EXTRA_ABS_COLS = 192
+LATE_EXTRA_ABS_COLS = 1280
 EXTRA_SCALE_COLS = 192
 HELD_AHEAD = 3
+DEFERRED = 3
 
 FLOPS = 2 * ROWS * K * N_OUT
 
@@ -118,11 +120,12 @@ def tile_modelnew_t_kernel(tc, x, weight, out):
             natural = natural_pool.tile([P, FLOW_COLS], BF16, name="natural")
             naturals[s] = natural
             first = s * CHUNK_COLS
-            nc.sync.dma_start(out=chunk[:, :K], in_=x_flat[:, first : first + K])
+            queue = nc.sync
+            queue.dma_start(out=chunk[:, :K], in_=x_flat[:, first : first + K])
             pieces = FLOW_TILES if s == 0 else 1
             width = FLOW_COLS // pieces
             for i in range(pieces):
-                nc.sync.dma_start(
+                queue.dma_start(
                     out=natural[:, i * width : (i + 1) * width],
                     in_=x_flat[:, first + K + i * width : first + K + (i + 1) * width],
                 )
@@ -144,11 +147,10 @@ def tile_modelnew_t_kernel(tc, x, weight, out):
             natural = naturals[s]
             magnitude = tree_pool.tile([P, CHUNK_COLS], BF16, name="magnitude")
             magnitudes[s] = magnitude
+            extra = LATE_EXTRA_ABS_COLS if s > CHUNKS - DEFERRED else EXTRA_ABS_COLS
             nc.scalar.activation(out=magnitude[:, :K], in_=grouped[s][:, :K], func=ACT.Abs)
-            nc.scalar.activation(
-                out=magnitude[:, K : K + EXTRA_ABS_COLS], in_=natural[:, :EXTRA_ABS_COLS], func=ACT.Abs
-            )
-            clear_signs(magnitude[:, K + EXTRA_ABS_COLS :], natural[:, EXTRA_ABS_COLS:])
+            nc.scalar.activation(out=magnitude[:, K : K + extra], in_=natural[:, :extra], func=ACT.Abs)
+            clear_signs(magnitude[:, K + extra :], natural[:, extra:])
 
         def fold_half(s):
             magnitude = magnitudes[s]
@@ -185,7 +187,7 @@ def tile_modelnew_t_kernel(tc, x, weight, out):
         first_fold(1)
         first_mask(3)
         first_fold(2)
-        clear_signs(w_abs[:], w_flat)
+        nc.scalar.activation(out=w_abs[:], in_=w_flat, func=ACT.Abs)
         first_fold(3)
         nc.vector.tensor_tensor(out=w_half[:], in0=w_abs[:, : K // 2], in1=w_abs[:, K // 2 :], op=ALU.max)
         nc.vector.reduce_max(out=w_column[:], in_=w_half[:], axis=AX.X)
@@ -196,7 +198,8 @@ def tile_modelnew_t_kernel(tc, x, weight, out):
             if s >= 2:
                 fold_half(s - 1)
             magnitude_of(s)
-            copy_out(s - 1)
+            if s - 1 < CHUNKS - DEFERRED:
+                copy_out(s - 1)
             if s == 1:
                 w_facts["inverse_scale"] = inverse_scale_of(w_turned, "w")
             if s >= 2:
@@ -205,7 +208,8 @@ def tile_modelnew_t_kernel(tc, x, weight, out):
                 w_facts["scale"] = reciprocal_of(w_facts["inverse_scale"], "w")
             if s >= 3:
                 fold_running(quarters[s - 2][:])
-        copy_out(CHUNKS - 1)
+        for s in range(CHUNKS - DEFERRED, CHUNKS):
+            copy_out(s)
 
         def transpose_held(c):
             held_banks[c] = transpose_tile(grouped[c][:, :K].bitcast(F32))

from contextlib import ExitStack

import concourse.mybir as mybir
from concourse.masks import make_identity

F32 = mybir.dt.float32
BF16 = mybir.dt.bfloat16
I32 = mybir.dt.int32
U32 = mybir.dt.uint32
U8 = mybir.dt.uint8
FP8X4 = mybir.dt.float8_e4m3fn_x4
ALU = mybir.AluOpType
ACT = mybir.ActivationFunctionType
AX = mybir.AxisListType

P = 128
ROWS = 8192
K = 1024
N_OUT = 128
ROW_TILES = ROWS // P
TILES_PER_CHUNK = 4
CHUNKS = ROW_TILES // TILES_PER_CHUNK
CHUNK_COLS = TILES_PER_CHUNK * K
FLOW_TILES = TILES_PER_CHUNK - 1
FLOW_COLS = FLOW_TILES * K
PASSES = K // 512
WORDS = K // 2
ABS_MASK = 0x7FFF7FFF
FP8_MAX = 448.0
EPS = 1e-12
EXTRA_ABS_COLS = 192
LATE_EXTRA_ABS_COLS = 1280
EXTRA_SCALE_COLS = 192
HELD_AHEAD = 3
DEFERRED = 3

FLOPS = 2 * ROWS * K * N_OUT


def tile_modelnew_t_kernel(tc, x, weight, out):
    nc = tc.nc
    x_flat = x.flatten_outer_dims().rearrange("(p t) k -> p (t k)", t=ROW_TILES)
    out_flat = out.flatten_outer_dims().rearrange("(p t) n -> p (t n)", t=ROW_TILES)

    with ExitStack() as stack:
        keep = stack.enter_context(tc.tile_pool(name="keep", bufs=1))
        natural_pool = stack.enter_context(tc.tile_pool(name="natural", bufs=4))
        tree_pool = stack.enter_context(tc.tile_pool(name="tree", bufs=2))
        mx_pool = stack.enter_context(tc.tile_pool(name="mx", bufs=3))
        result_pool = stack.enter_context(tc.tile_pool(name="result", bufs=3))
        banks = stack.enter_context(tc.psum_pool(name="banks", bufs=8))
        stack.enter_context(tc.manual_schedule())

        identity = keep.tile([P, P], F32)
        make_identity(nc, identity[:])
        over_448 = keep.tile([P, P], F32)
        nc.vector.memset(over_448[:], 1.0 / FP8_MAX)
        running = keep.tile([P, K], BF16)
        nc.vector.memset(running[:], 0.0)

        def spread(column, name):
            repeated = keep.tile([P, P], F32, name=name + "_repeated")
            nc.vector.tensor_scalar(
                out=repeated[:], in0=over_448[:], scalar1=column[:, 0:1], scalar2=EPS / FP8_MAX, op0=ALU.mult, op1=ALU.max
            )
            turned = banks.tile([P, P], F32, name=name + "_turned", tag="bank")
            nc.tensor.transpose(turned[:], repeated[:], identity[:])
            return turned

        def inverse_scale_of(turned, name):
            inverse_scale = keep.tile([P, 1], F32, name=name + "_inverse_scale")
            nc.vector.reduce_max(out=inverse_scale[:], in_=turned[:], axis=AX.X)
            return inverse_scale

        def reciprocal_of(inverse_scale, name):
            the_scale = keep.tile([P, 1], F32, name=name + "_scale")
            nc.vector.reciprocal(out=the_scale[:], in_=inverse_scale[:])
            return the_scale

        def clear_signs(out_cols, in_cols):
            nc.vector.tensor_scalar(
                out=out_cols.bitcast(I32), in0=in_cols.bitcast(I32), scalar1=ABS_MASK, scalar2=None, op0=ALU.bitwise_and
            )

        def transpose_tile(words):
            flipped = banks.tile([P, WORDS], F32, name="flipped", tag="bank")
            for a in range(2 * PASSES):
                nc.tensor.transpose(flipped[:, a * P : (a + 1) * P], words[:, a * P : (a + 1) * P], identity[:])
            return flipped

        w_raw = keep.tile([P, 2 * PASSES, 2 * N_OUT], BF16)
        w_flat = w_raw[:].rearrange("p a c -> p (a c)")
        w_abs = keep.tile([P, K], BF16)
        w_half = keep.tile([P, K // 2], BF16)
        w_column = keep.tile([P, 1], F32)
        w_grouped = keep.tile([P, PASSES, N_OUT, 4], BF16, align_bytes=64)
        w_codes = keep.tile([P, PASSES * N_OUT], U32, align_bytes=64)
        w_scales = keep.tile([P, PASSES * N_OUT], U8, align_bytes=64)

        def weight_group(g, w_scale):
            nc.vector.tensor_scalar(
                out=w_grouped[:, g].rearrange("p n (u e) -> p n u e", u=2),
                in0=w_raw[:, 2 * g : 2 * g + 2, :].rearrange("p u (e n) -> p n u e", e=2),
                scalar1=w_scale[:, 0:1],
                scalar2=None,
                op0=ALU.mult,
            )

        grouped = []
        naturals = {}
        magnitudes = {}
        halves = {}
        quarters = {}
        flow_banks = {}
        held_banks = {}

        def load_and_transpose(s):
            chunk = keep.tile([P, CHUNK_COLS], BF16, name="grouped%d" % s, align_bytes=64)
            grouped.append(chunk)
            natural = natural_pool.tile([P, FLOW_COLS], BF16, name="natural")
            naturals[s] = natural
            first = s * CHUNK_COLS
            queue = nc.sync
            queue.dma_start(out=chunk[:, :K], in_=x_flat[:, first : first + K])
            pieces = FLOW_TILES if s == 0 else 1
            width = FLOW_COLS // pieces
            for i in range(pieces):
                queue.dma_start(
                    out=natural[:, i * width : (i + 1) * width],
                    in_=x_flat[:, first + K + i * width : first + K + (i + 1) * width],
                )
            words = natural[:].bitcast(F32)
            for t in range(FLOW_TILES):
                flow_banks[(s, t)] = transpose_tile(words[:, t * WORDS : (t + 1) * WORDS])

        def copy_out(s):
            chunk_words = grouped[s][:].bitcast(F32).rearrange(
                "p (t g r u) -> p t g r u", t=TILES_PER_CHUNK, g=PASSES, r=P, u=2
            )
            for t in range(FLOW_TILES):
                nc.scalar.copy(
                    out=chunk_words[:, t + 1],
                    in_=flow_banks[(s, t)][:].rearrange("p (g u r) -> p g r u", g=PASSES, u=2, r=P),
                )

        def magnitude_of(s):
            natural = naturals[s]
            magnitude = tree_pool.tile([P, CHUNK_COLS], BF16, name="magnitude")
            magnitudes[s] = magnitude
            extra = LATE_EXTRA_ABS_COLS if s > CHUNKS - DEFERRED else EXTRA_ABS_COLS
            nc.scalar.activation(out=magnitude[:, :K], in_=grouped[s][:, :K], func=ACT.Abs)
            nc.scalar.activation(out=magnitude[:, K : K + extra], in_=natural[:, :extra], func=ACT.Abs)
            clear_signs(magnitude[:, K + extra :], natural[:, extra:])

        def fold_half(s):
            magnitude = magnitudes[s]
            half = tree_pool.tile([P, CHUNK_COLS // 2], BF16, name="half")
            halves[s] = half
            nc.vector.tensor_tensor(
                out=half[:], in0=magnitude[:, : CHUNK_COLS // 2], in1=magnitude[:, CHUNK_COLS // 2 :], op=ALU.max
            )

        def fold_quarter(s):
            half = halves[s]
            quarter = tree_pool.tile([P, K], BF16, name="quarter")
            quarters[s] = quarter
            nc.vector.tensor_tensor(out=quarter[:], in0=half[:, :K], in1=half[:, K:], op=ALU.max)

        def fold_running(values):
            nc.vector.tensor_tensor(out=running[:], in0=running[:], in1=values, op=ALU.max)

        load_and_transpose(0)
        nc.sync.dma_start(out=w_raw[:], in_=weight.rearrange("(a p e) n -> p a (e n)", a=2 * PASSES, p=P, e=2))
        first_magnitude = tree_pool.tile([P, CHUNK_COLS], BF16, name="magnitude")

        def first_mask(i):
            source = grouped[0][:, :K] if i == 0 else naturals[0][:, (i - 1) * K : i * K]
            clear_signs(first_magnitude[:, i * K : (i + 1) * K], source)

        def first_fold(i):
            fold_running(first_magnitude[:, i * K : (i + 1) * K])

        first_mask(0)
        first_mask(1)
        first_fold(0)
        first_mask(2)
        first_fold(1)
        first_mask(3)
        first_fold(2)
        nc.scalar.activation(out=w_abs[:], in_=w_flat, func=ACT.Abs)
        first_fold(3)
        nc.vector.tensor_tensor(out=w_half[:], in0=w_abs[:, : K // 2], in1=w_abs[:, K // 2 :], op=ALU.max)
        nc.vector.reduce_max(out=w_column[:], in_=w_half[:], axis=AX.X)
        w_turned = spread(w_column, "w")
        w_facts = {}
        for s in range(1, CHUNKS):
            load_and_transpose(s)
            if s >= 2:
                fold_half(s - 1)
            magnitude_of(s)
            if s - 1 < CHUNKS - DEFERRED:
                copy_out(s - 1)
            if s == 1:
                w_facts["inverse_scale"] = inverse_scale_of(w_turned, "w")
            if s >= 2:
                fold_quarter(s - 1)
            if s == 2:
                w_facts["scale"] = reciprocal_of(w_facts["inverse_scale"], "w")
            if s >= 3:
                fold_running(quarters[s - 2][:])
        for s in range(CHUNKS - DEFERRED, CHUNKS):
            copy_out(s)

        def transpose_held(c):
            held_banks[c] = transpose_tile(grouped[c][:, :K].bitcast(F32))

        for c in range(HELD_AHEAD):
            transpose_held(c)
        fold_half(CHUNKS - 1)
        fold_running(quarters[CHUNKS - 2][:])
        fold_quarter(CHUNKS - 1)
        fold_running(quarters[CHUNKS - 1][:])
        x_column = keep.tile([P, 1], F32)
        nc.vector.reduce_max(out=x_column[:], in_=running[:], axis=AX.X)
        x_turned = spread(x_column, "x")
        weight_group(0, w_facts["scale"])
        weight_group(1, w_facts["scale"])
        x_inverse_scale = inverse_scale_of(x_turned, "x")
        nc.vector.quantize_mx(
            out=w_codes[:].bitcast(FP8X4), scales=w_scales[:], in_=w_grouped[:].rearrange("p g n j -> p (g n j)")
        )
        x_scale = reciprocal_of(x_inverse_scale, "x")
        final_factor = keep.tile([P, 1], F32)
        nc.vector.tensor_tensor(out=final_factor[:], in0=x_inverse_scale[:], in1=w_facts["inverse_scale"][:], op=ALU.mult)

        def scale(c):
            flat = grouped[c]
            pairs = held_banks[c][:].bitcast(BF16)
            for g in range(PASSES):
                cols = slice(g * 512, (g + 1) * 512)
                nc.scalar.activation(
                    out=flat[:, cols].rearrange("p (r u e) -> p r u e", r=P, u=2, e=2),
                    in_=pairs[:, cols].rearrange("p (u r e) -> p r u e", u=2, r=P, e=2),
                    func=ACT.Copy,
                    scale=x_scale[:, 0:1],
                )
            split = K + EXTRA_SCALE_COLS
            nc.scalar.activation(out=flat[:, K:split], in_=flat[:, K:split], func=ACT.Copy, scale=x_scale[:, 0:1])
            nc.vector.tensor_scalar(
                out=flat[:, split:], in0=flat[:, split:], scalar1=x_scale[:, 0:1], scalar2=None, op0=ALU.mult
            )

        def multiply(c, first_tile, tiles):
            width = tiles * K
            codes = mx_pool.tile([P, width // 4], U32, name="codes", align_bytes=64)
            scales = mx_pool.tile([P, width // 4], U8, name="scales", align_bytes=64)
            nc.vector.quantize_mx(
                out=codes[:].bitcast(FP8X4), scales=scales[:], in_=grouped[c][:, first_tile * K : first_tile * K + width]
            )
            acc = banks.tile([P, tiles, N_OUT], F32, name="acc", tag="bank")
            for t in range(tiles):
                for g in range(PASSES):
                    x_cols = slice((t * PASSES + g) * P, (t * PASSES + g + 1) * P)
                    w_cols = slice(g * N_OUT, (g + 1) * N_OUT)
                    nc.tensor.matmul_mx(
                        out=acc[:, t, :],
                        lhsT=codes[:, x_cols].bitcast(FP8X4),
                        lhsT_scale=scales[:, x_cols],
                        rhs=w_codes[:, w_cols].bitcast(FP8X4),
                        rhs_scale=w_scales[:, w_cols],
                        start=(g == 0),
                        stop=(g == PASSES - 1),
                    )
            return acc

        def finish(c, first_tile, tiles, acc):
            width = tiles * N_OUT
            if tiles == TILES_PER_CHUNK:
                result = result_pool.tile([P, width], F32, name="result")
            else:
                result = keep.tile([P, width], F32, name="piece%d" % first_tile)
            nc.scalar.activation(
                out=result[:], in_=acc[:].rearrange("p t n -> p (t n)"), func=ACT.Copy, scale=final_factor[:, 0:1]
            )
            first_col = (c * TILES_PER_CHUNK + first_tile) * N_OUT
            nc.sync.dma_start(out=out_flat[:, first_col : first_col + width], in_=result[:])

        scale(0)
        scale(1)
        products = {}
        for c in range(CHUNKS - 1):
            products[c] = multiply(c, 0, TILES_PER_CHUNK)
            if c + HELD_AHEAD < CHUNKS:
                transpose_held(c + HELD_AHEAD)
            if c + 2 < CHUNKS:
                scale(c + 2)
            if c >= 1:
                finish(c - 1, 0, TILES_PER_CHUNK, products[c - 1])
        last = CHUNKS - 1
        for t in range(TILES_PER_CHUNK):
            products[(last, t)] = multiply(last, t, 1)
            if t == 0:
                finish(last - 1, 0, TILES_PER_CHUNK, products[last - 1])
            else:
                finish(last, t - 1, 1, products[(last, t - 1)])
        finish(last, TILES_PER_CHUNK - 1, 1, products[(last, TILES_PER_CHUNK - 1)])
